import numpy as np
import ml_dtypes


def mxq(x, axis, fmt="e4m3"):
    dtype, down = {"e4m3": (ml_dtypes.float8_e4m3fn, 7), "e5m2": (ml_dtypes.float8_e5m2, 14)}[fmt]
    v = np.moveaxis(np.asarray(x, np.float32).astype(ml_dtypes.bfloat16).astype(np.float64), axis, -1)
    blocks = v.reshape(v.shape[:-1] + (-1, 32))
    amax = np.abs(blocks).max(-1, keepdims=True)
    byte = np.maximum(np.where(amax > 0, np.frexp(amax)[1] - 1 + 127, 0) - down, 1)
    scale = np.exp2(byte - 127.0)
    codes = (blocks / scale).astype(np.float32).astype(dtype).astype(np.float64)
    return np.moveaxis((codes * scale).reshape(v.shape), -1, axis)


WIDE = False


def mx_kscale(k):
    if not WIDE:
        return np.ones(k)
    levels = np.array([10, -10, 5, -5, 0])
    a = np.random.permutation(np.resize(levels, k // 512 * 4)).reshape(k // 512, 4)
    idx = np.arange(k)
    return np.exp2(a[idx // 512, idx % 128 // 32])


BF16 = ml_dtypes.bfloat16


def bf(x):
    return np.asarray(x, np.float32).astype(BF16)


def f64(x):
    return np.asarray(x).astype(np.float64)


E2M1 = np.array([0.0, 0.5, 1.0, 1.5, 2.0, 3.0, 4.0, 6.0, -0.0, -0.5, -1.0, -1.5, -2.0, -3.0, -4.0, -6.0])


def pack_weight(w, fmt):
    k, n = w.shape
    w = f64(bf(w)).reshape(k // 32, 32, n)
    amax = np.abs(w).max(1)
    if fmt == "e4m3":
        byte = np.frexp(amax)[1] - 1 + 127 - 7
    else:
        mant, ex = np.frexp(amax / 6.0)
        byte = np.where(mant > 0.5, ex, ex - 1) + 127
    byte = np.clip(np.where(amax > 0, byte, 1), 1, 254)
    scaled = (w * np.exp2(127.0 - byte)[:, None, :]).reshape(k, n).astype(np.float32)
    by_word = np.ascontiguousarray(scaled.reshape(k // 512, 128, 4, n).transpose(0, 1, 3, 2))
    if fmt == "e4m3":
        words = by_word.astype(ml_dtypes.float8_e4m3fn).view(np.uint8)
    else:
        c = by_word.astype(ml_dtypes.float4_e2m1fn).view(np.uint8) & 0xF
        words = c[..., 0::2] | (c[..., 1::2] << 4)
    return np.ascontiguousarray(words), np.ascontiguousarray(byte.astype(np.uint8).reshape(k // 512, 16, n))


def unpack_weight(words, scales, fmt):
    g, p, n, _ = words.shape
    if fmt == "e4m3":
        vals = np.ascontiguousarray(words).view(ml_dtypes.float8_e4m3fn).astype(np.float64)
    else:
        nib = np.empty((g, p, n, 4), np.uint8)
        nib[..., 0::2] = words & 0xF
        nib[..., 1::2] = words >> 4
        vals = E2M1[nib]
    vals = vals * np.repeat(np.exp2(scales.astype(np.float64) - 127.0), 8, axis=1)[..., None]
    return vals.transpose(0, 1, 3, 2).reshape(g * 512, n)


B, S, D, H, DH, F = 2, 128, 2048, 16, 128, 4096
E = H * DH
EPS = 1e-5
NTERMS = 120
FMT = "e4m3"


def layernorm(x, g, b):
    mu = x.mean(-1, keepdims=True)
    var = np.square(x - mu).mean(-1, keepdims=True)
    return (x - mu) / np.sqrt(var + EPS) * g + b


def erf(v):
    a = np.minimum(np.maximum(v, -6.0), 6.0)
    term = a.copy()
    total = a.copy()
    for n in range(1, NTERMS):
        term = term * (2.0 * a * a) / (2.0 * n + 1.0)
        total = total + term
    return 2.0 / np.sqrt(np.pi) * np.exp(-a * a) * total


def gelu_erf(v):
    return 0.5 * v * (1.0 + erf(v / np.sqrt(2.0)))


def setup_inputs():
    s, t = mx_kscale(E), mx_kscale(D)
    x = np.random.standard_normal((B, S, D)) + 0.5 * np.random.standard_normal((B, S, 1))
    h_attn = bf(0.2 * np.random.standard_normal((B, S, E)) * s)
    w_out = np.random.standard_normal((D, E)) * 2.0 / np.sqrt(E) / s
    w_fc1 = np.random.standard_normal((F, D)) / np.sqrt(D) / t
    g2 = bf((1.0 + 0.1 * np.random.standard_normal(D)) * t)
    b2 = bf(0.1 * np.random.standard_normal(D) * t)
    w_out_words, w_out_scales = pack_weight(np.ascontiguousarray(w_out.T), FMT)
    w_fc1_words, w_fc1_scales = pack_weight(np.ascontiguousarray(w_fc1.T), FMT)
    return {"h_attn": h_attn,
            "x": bf(x),
            "w_out_words": w_out_words,
            "w_out_scales": w_out_scales,
            "w_fc1_words": w_fc1_words,
            "w_fc1_scales": w_fc1_scales,
            "g2": g2,
            "b2": b2}


def reference(h_attn, x, w_out_words, w_out_scales, w_fc1_words, w_fc1_scales, g2, b2):
    x_mid = f64(x) + (mxq(f64(h_attn), 2, "e4m3") @ unpack_weight(w_out_words, w_out_scales, FMT))
    h = layernorm(x_mid, f64(g2), f64(b2))
    u = mxq(h, 2, "e4m3") @ unpack_weight(w_fc1_words, w_fc1_scales, FMT)
    return x_mid, gelu_erf(u)

@@ -1,0 +1,233 @@
+import concourse.mybir as mybir
+from concourse.masks import make_identity
+
+BF16 = mybir.dt.bfloat16
+F32 = mybir.dt.float32
+I32 = mybir.dt.int32
+U32 = mybir.dt.uint32
+U8 = mybir.dt.uint8
+FP8X4 = mybir.dt.float8_e4m3fn_x4
+ALU = mybir.AluOpType
+ACT = mybir.ActivationFunctionType
+
+P = 128
+PACK = 4
+K_PASS = P * PACK
+TOKEN_TILES = 2
+D = 2048
+F = 4096
+PASSES = D // K_PASS
+N_TILE = 512
+BLOCK = 1024
+TILES_PER_BLOCK = BLOCK // N_TILE
+QUADRANT = 32
+EPS = 1e-5
+LAG = 2
+
+FLOPS = 2 * TOKEN_TILES * P * D * (D + F)
+
+
+def load_scale_planes(nc, planes, scales):
+    for quadrant in range(P // QUADRANT):
+        first = QUADRANT * quadrant
+        nc.sync.dma_start(
+            out=planes[first : first + PACK * PASSES, :].bitcast(I32),
+            in_=scales[:, PACK * quadrant : PACK * (quadrant + 1), :].bitcast(I32),
+        )
+
+
+def load_weight_block(nc, w_sb, words, col0):
+    for g in range(PASSES):
+        rows = words[g].rearrange("p n t -> p (n t)")
+        nc.sync.dma_start(
+            out=w_sb[:, g, col0 : col0 + BLOCK].bitcast(I32),
+            in_=rows[:, PACK * col0 : PACK * (col0 + BLOCK)].bitcast(I32),
+        )
+
+
+def flip_and_quantise(nc, flip_banks, stage, identity, src, codes, planes):
+    pairs = src[:].bitcast(F32)
+    pairs_per_pass = K_PASS // 2
+    for half in range(PASSES // 2):
+        flipped = flip_banks.tile([P, 2, 2, P], F32, name="flipped")
+        for i in range(2):
+            g = 2 * half + i
+            for u in range(2):
+                nc.tensor.transpose(
+                    flipped[:, i, u, :],
+                    pairs[:, pairs_per_pass * g + u : pairs_per_pass * (g + 1) : 2],
+                    identity[:],
+                )
+        grouped = stage.tile([P, 2, P, PACK], BF16, name="grouped", align_bytes=64)
+        nc.scalar.copy(out=grouped[:].bitcast(F32), in_=flipped[:].rearrange("p g u r -> p g r u"))
+        cols = slice(2 * P * half, 2 * P * (half + 1))
+        nc.vector.quantize_mx(
+            out=codes[:, cols].bitcast(FP8X4),
+            scales=planes[:, cols],
+            in_=grouped[:].rearrange("p g r t -> p (g r t)"),
+        )
+
+
+def mx_pass(nc, sums, g, codes, planes, w_sb, w_planes, col0):
+    tokens = slice(P * g, P * (g + 1))
+    cols = slice(col0, col0 + N_TILE)
+    nc.tensor.matmul_mx(
+        out=sums[:],
+        lhsT=codes[:, tokens].bitcast(FP8X4),
+        lhsT_scale=planes[:, tokens],
+        rhs=w_sb[:, g, cols].bitcast(FP8X4),
+        rhs_scale=w_planes[PACK * g : P, cols],
+        start=(g == 0),
+        stop=(g == PASSES - 1),
+    )
+
+
+def tile_minitransformerlayer_pb_kernel(
+    tc, h_attn, x, w_out_words, w_out_scales, w_fc1_words, w_fc1_scales, g2, b2, out_0, out_1
+):
+    nc = tc.nc
+    with (
+        tc.tile_pool(name="resident", bufs=1) as resident,
+        tc.tile_pool(name="stage", bufs=2) as stage,
+        tc.tile_pool(name="results", bufs=4) as results,
+        tc.psum_pool(name="flip_banks", bufs=2) as flip_banks,
+        tc.psum_pool(name="sum_banks", bufs=6) as sum_banks,
+    ):
+        token_tiles = range(TOKEN_TILES)
+
+        w_out_sb = resident.tile([P, PASSES, D], U32, align_bytes=64)
+        w_fc1_sb = resident.tile([P, PASSES, F], U32, align_bytes=64)
+        w_out_planes = resident.tile([P, D], U8, align_bytes=64)
+        w_fc1_planes = resident.tile([P, F], U8, align_bytes=64)
+        attn_sb = [resident.tile([P, D], BF16, name="attn_sb%d" % m) for m in token_tiles]
+        x_sb = [resident.tile([P, D], BF16, name="x_sb%d" % m) for m in token_tiles]
+        x_mid = [resident.tile([P, D], F32, name="x_mid%d" % m) for m in token_tiles]
+        h_sb = [resident.tile([P, D], BF16, name="h_sb%d" % m) for m in token_tiles]
+        attn_codes = [resident.tile([P, D // PACK], U32, name="attn_codes%d" % m, align_bytes=64) for m in token_tiles]
+        attn_planes = [resident.tile([P, D // PACK], U8, name="attn_planes%d" % m, align_bytes=64) for m in token_tiles]
+        h_codes = [resident.tile([P, D // PACK], U32, name="h_codes%d" % m, align_bytes=64) for m in token_tiles]
+        h_planes = [resident.tile([P, D // PACK], U8, name="h_planes%d" % m, align_bytes=64) for m in token_tiles]
+        row_sums = [resident.tile([P, D // N_TILE], F32, name="row_sums%d" % m) for m in token_tiles]
+        neg_mean = [resident.tile([P, 1], F32, name="neg_mean%d" % m) for m in token_tiles]
+        sq_sum = [resident.tile([P, 1], F32, name="sq_sum%d" % m) for m in token_tiles]
+        std = [resident.tile([P, 1], F32, name="std%d" % m) for m in token_tiles]
+        rstd = [resident.tile([P, 1], F32, name="rstd%d" % m) for m in token_tiles]
+        gain_bias_row = resident.tile([P, 2 * D], BF16)
+        gain_bias = resident.tile([P, 2 * D], BF16)
+        ones = resident.tile([P, P], BF16)
+        identity = resident.tile([P, P], F32)
+        eps = resident.tile([P, 1], F32)
+        warm = resident.tile([P, 1], F32)
+
+        nc.vector.memset(w_out_planes[:].bitcast(I32), 0)
+        nc.vector.memset(gain_bias_row[:].bitcast(I32), 0)
+        nc.vector.memset(w_fc1_planes[:].bitcast(I32), 0)
+        nc.vector.memset(ones[:], 1.0)
+        nc.vector.memset(eps[:], EPS)
+        make_identity(nc, identity[:])
+        nc.scalar.activation(out=warm[:], in_=eps[:], func=ACT.Sqrt)
+
+        nc.scalar.dma_start(out=gain_bias_row[0:1, 0:D], in_=g2.rearrange("(o d) -> o d", o=1))
+        nc.scalar.dma_start(out=gain_bias_row[0:1, D : 2 * D], in_=b2.rearrange("(o d) -> o d", o=1))
+        for m in token_tiles:
+            nc.sync.dma_start(out=attn_sb[m][:], in_=h_attn[m])
+        load_scale_planes(nc, w_out_planes, w_out_scales)
+        load_weight_block(nc, w_out_sb, w_out_words, 0)
+        for m in token_tiles:
+            nc.sync.dma_start(out=x_sb[m][:], in_=x[m])
+        for col0 in range(BLOCK, D, BLOCK):
+            load_weight_block(nc, w_out_sb, w_out_words, col0)
+        load_scale_planes(nc, w_fc1_planes, w_fc1_scales)
+        for col0 in range(0, F, BLOCK):
+            load_weight_block(nc, w_fc1_sb, w_fc1_words, col0)
+
+        for m in token_tiles:
+            flip_and_quantise(nc, flip_banks, stage, identity, attn_sb[m], attn_codes[m], attn_planes[m])
+
+        for col0 in range(0, 2 * D, 2 * N_TILE):
+            spread = sum_banks.tile([P, 2 * N_TILE], BF16, name="spread", tag="bank")
+            for i in range(2):
+                cols = slice(col0 + N_TILE * i, col0 + N_TILE * (i + 1))
+                nc.tensor.matmul(
+                    out=spread[:, N_TILE * i : N_TILE * (i + 1)],
+                    lhsT=ones[:],
+                    rhs=gain_bias_row[:, cols],
+                    start=True,
+                    stop=True,
+                )
+            nc.scalar.copy(out=gain_bias[:, col0 : col0 + 2 * N_TILE], in_=spread[:])
+        gain = gain_bias[:, 0:D]
+        bias = gain_bias[:, D : 2 * D]
+
+        for col0 in range(0, D, BLOCK):
+            sums = [
+                [sum_banks.tile([P, N_TILE], F32, name="sums", tag="bank") for c in range(TILES_PER_BLOCK)]
+                for m in token_tiles
+            ]
+            for g in range(PASSES):
+                for m in token_tiles:
+                    for c in range(TILES_PER_BLOCK):
+                        mx_pass(
+                            nc, sums[m][c], g, attn_codes[m], attn_planes[m],
+                            w_out_sb, w_out_planes, col0 + N_TILE * c,
+                        )
+            for m in token_tiles:
+                for c in range(TILES_PER_BLOCK):
+                    first = col0 + N_TILE * c
+                    cols = slice(first, first + N_TILE)
+                    nc.vector.scalar_tensor_tensor(
+                        out=x_mid[m][:, cols],
+                        in0=sums[m][c][:],
+                        scalar=1.0,
+                        in1=x_sb[m][:, cols],
+                        op0=ALU.mult,
+                        op1=ALU.add,
+                        accum_out=row_sums[m][:, first // N_TILE : first // N_TILE + 1],
+                    )
+
+        for m in token_tiles:
+            nc.sync.dma_start(out=out_0[m], in_=x_mid[m][:])
+            total = stage.tile([P, 1], F32, name="total")
+            nc.vector.tensor_reduce(out=total[:], in_=row_sums[m][:], axis=mybir.AxisListType.X, op=ALU.add)
+            nc.vector.tensor_scalar_mul(out=neg_mean[m][:], in0=total[:], scalar1=-1.0 / D)
+            squares = stage.tile([P, D], BF16, name="squares")
+            nc.scalar.activation(
+                out=squares[:], in_=x_mid[m][:], func=ACT.Square, bias=neg_mean[m][:], scale=1.0,
+                accum_out=sq_sum[m][:],
+            )
+            nc.scalar.activation(out=std[m][:], in_=sq_sum[m][:], func=ACT.Sqrt, bias=eps[:], scale=1.0 / D)
+
+        for m in token_tiles:
+            centred = stage.tile([P, D], F32, name="centred")
+            nc.vector.scalar_tensor_tensor(
+                out=centred[:], in0=x_mid[m][:], scalar=neg_mean[m][:], in1=gain, op0=ALU.add, op1=ALU.mult
+            )
+            nc.vector.reciprocal(out=rstd[m][:], in_=std[m][:])
+            for col0 in range(0, D, BLOCK):
+                cols = slice(col0, col0 + BLOCK)
+                nc.vector.scalar_tensor_tensor(
+                    out=h_sb[m][:, cols], in0=centred[:, cols], scalar=rstd[m][:], in1=bias[:, cols],
+                    op0=ALU.mult, op1=ALU.add,
+                )
+
+        blocks = F // BLOCK
+        for step in range(blocks + LAG * (TOKEN_TILES - 1)):
+            for m in token_tiles:
+                block = step - LAG * m
+                if block == 0:
+                    flip_and_quantise(nc, flip_banks, stage, identity, h_sb[m], h_codes[m], h_planes[m])
+                if 0 <= block < blocks:
+                    col0 = BLOCK * block
+                    sums = [sum_banks.tile([P, N_TILE], F32, name="sums", tag="bank") for c in range(TILES_PER_BLOCK)]
+                    for g in range(PASSES):
+                        for c in range(TILES_PER_BLOCK):
+                            mx_pass(
+                                nc, sums[c], g, h_codes[m], h_planes[m],
+                                w_fc1_sb, w_fc1_planes, col0 + N_TILE * c,
+                            )
+                    act_sb = results.tile([P, BLOCK], F32, name="act_sb")
+                    for c in range(TILES_PER_BLOCK):
+                        nc.scalar.activation(
+                            out=act_sb[:, N_TILE * c : N_TILE * (c + 1)], in_=sums[c][:], func=ACT.Gelu
+                        )
+                    nc.sync.dma_start(out=out_1[m][:, col0 : col0 + BLOCK], in_=act_sb[:])

@@ -92,6 +92,7 @@ def tile_minitransformerlayer_pb_kernel(
         tc.tile_pool(name="results", bufs=4) as results,
         tc.psum_pool(name="flip_banks", bufs=2) as flip_banks,
         tc.psum_pool(name="sum_banks", bufs=6) as sum_banks,
+        tc.manual_schedule(),
     ):
         token_tiles = range(TOKEN_TILES)
 
@@ -119,11 +120,11 @@ def tile_minitransformerlayer_pb_kernel(
         eps = resident.tile([P, 1], F32)
         warm = resident.tile([P, 1], F32)
 
+        nc.vector.memset(eps[:], EPS)
         nc.vector.memset(w_out_planes[:].bitcast(I32), 0)
         nc.vector.memset(gain_bias_row[:].bitcast(I32), 0)
-        nc.vector.memset(w_fc1_planes[:].bitcast(I32), 0)
         nc.vector.memset(ones[:], 1.0)
-        nc.vector.memset(eps[:], EPS)
+        nc.vector.memset(w_fc1_planes[:].bitcast(I32), 0)
         make_identity(nc, identity[:])
         nc.scalar.activation(out=warm[:], in_=eps[:], func=ACT.Sqrt)
 
@@ -171,6 +172,7 @@ def tile_minitransformerlayer_pb_kernel(
                             nc, sums[m][c], g, attn_codes[m], attn_planes[m],
                             w_out_sb, w_out_planes, col0 + N_TILE * c,
                         )
+            last_block = col0 + BLOCK == D
             for m in token_tiles:
                 for c in range(TILES_PER_BLOCK):
                     first = col0 + N_TILE * c
@@ -184,50 +186,56 @@ def tile_minitransformerlayer_pb_kernel(
                         op1=ALU.add,
                         accum_out=row_sums[m][:, first // N_TILE : first // N_TILE + 1],
                     )
-
-        for m in token_tiles:
-            nc.sync.dma_start(out=out_0[m], in_=x_mid[m][:])
-            total = stage.tile([P, 1], F32, name="total")
-            nc.vector.tensor_reduce(out=total[:], in_=row_sums[m][:], axis=mybir.AxisListType.X, op=ALU.add)
-            nc.vector.tensor_scalar_mul(out=neg_mean[m][:], in0=total[:], scalar1=-1.0 / D)
-            squares = stage.tile([P, D], BF16, name="squares")
-            nc.scalar.activation(
-                out=squares[:], in_=x_mid[m][:], func=ACT.Square, bias=neg_mean[m][:], scale=1.0,
-                accum_out=sq_sum[m][:],
-            )
-            nc.scalar.activation(out=std[m][:], in_=sq_sum[m][:], func=ACT.Sqrt, bias=eps[:], scale=1.0 / D)
-
-        for m in token_tiles:
-            centred = stage.tile([P, D], F32, name="centred")
-            nc.vector.scalar_tensor_tensor(
-                out=centred[:], in0=x_mid[m][:], scalar=neg_mean[m][:], in1=gain, op0=ALU.add, op1=ALU.mult
-            )
-            nc.vector.reciprocal(out=rstd[m][:], in_=std[m][:])
-            for col0 in range(0, D, BLOCK):
-                cols = slice(col0, col0 + BLOCK)
-                nc.vector.scalar_tensor_tensor(
-                    out=h_sb[m][:, cols], in0=centred[:, cols], scalar=rstd[m][:], in1=bias[:, cols],
-                    op0=ALU.mult, op1=ALU.add,
-                )
+                if last_block:
+                    nc.sync.dma_start(out=out_0[m], in_=x_mid[m][:])
+                    total = stage.tile([P, 1], F32, name="total")
+                    nc.vector.tensor_reduce(
+                        out=total[:], in_=row_sums[m][:], axis=mybir.AxisListType.X, op=ALU.add
+                    )
+                    nc.vector.tensor_scalar_mul(out=neg_mean[m][:], in0=total[:], scalar1=-1.0 / D)
+                    squares = stage.tile([P, D], BF16, name="squares")
+                    nc.scalar.activation(
+                        out=squares[:], in_=x_mid[m][:], func=ACT.Square, bias=neg_mean[m][:], scale=1.0,
+                        accum_out=sq_sum[m][:],
+                    )
+                    nc.scalar.activation(
+                        out=std[m][:], in_=sq_sum[m][:], func=ACT.Sqrt, bias=eps[:], scale=1.0 / D
+                    )
 
         blocks = F // BLOCK
         for step in range(blocks + LAG * (TOKEN_TILES - 1)):
             for m in token_tiles:
-                block = step - LAG * m
-                if block == 0:
+                if step == LAG * m:
+                    centred = stage.tile([P, D], F32, name="centred")
+                    nc.vector.scalar_tensor_tensor(
+                        out=centred[:], in0=x_mid[m][:], scalar=neg_mean[m][:], in1=gain,
+                        op0=ALU.add, op1=ALU.mult,
+                    )
+                    nc.vector.reciprocal(out=rstd[m][:], in_=std[m][:])
+                    for col0 in range(0, D, BLOCK):
+                        cols = slice(col0, col0 + BLOCK)
+                        nc.vector.scalar_tensor_tensor(
+                            out=h_sb[m][:, cols], in0=centred[:, cols], scalar=rstd[m][:], in1=bias[:, cols],
+                            op0=ALU.mult, op1=ALU.add,
+                        )
                     flip_and_quantise(nc, flip_banks, stage, identity, h_sb[m], h_codes[m], h_planes[m])
+            for m in token_tiles:
+                block = step - LAG * m
                 if 0 <= block < blocks:
                     col0 = BLOCK * block
-                    sums = [sum_banks.tile([P, N_TILE], F32, name="sums", tag="bank") for c in range(TILES_PER_BLOCK)]
+                    products = [
+                        sum_banks.tile([P, N_TILE], F32, name="products", tag="bank")
+                        for c in range(TILES_PER_BLOCK)
+                    ]
                     for g in range(PASSES):
                         for c in range(TILES_PER_BLOCK):
                             mx_pass(
-                                nc, sums[c], g, h_codes[m], h_planes[m],
+                                nc, products[c], g, h_codes[m], h_planes[m],
                                 w_fc1_sb, w_fc1_planes, col0 + N_TILE * c,
                             )
                     act_sb = results.tile([P, BLOCK], F32, name="act_sb")
                     for c in range(TILES_PER_BLOCK):
                         nc.scalar.activation(
-                            out=act_sb[:, N_TILE * c : N_TILE * (c + 1)], in_=sums[c][:], func=ACT.Gelu
+                            out=act_sb[:, N_TILE * c : N_TILE * (c + 1)], in_=products[c][:], func=ACT.Gelu
                         )
                     nc.sync.dma_start(out=out_1[m][:, col0 : col0 + BLOCK], in_=act_sb[:])

@@ -36,12 +36,12 @@ def load_scale_planes(nc, planes, scales):
         )
 
 
-def load_weight_block(nc, w_sb, words, col0):
+def load_weight_block(nc, w_sb, words, col0, width):
     for g in range(PASSES):
         rows = words[g].rearrange("p n t -> p (n t)")
         nc.sync.dma_start(
-            out=w_sb[:, g, col0 : col0 + BLOCK].bitcast(I32),
-            in_=rows[:, PACK * col0 : PACK * (col0 + BLOCK)].bitcast(I32),
+            out=w_sb[:, g, col0 : col0 + width].bitcast(I32),
+            in_=rows[:, PACK * col0 : PACK * (col0 + width)].bitcast(I32),
         )
 
 
@@ -133,14 +133,14 @@ def tile_minitransformerlayer_pb_kernel(
         for m in token_tiles:
             nc.sync.dma_start(out=attn_sb[m][:], in_=h_attn[m])
         load_scale_planes(nc, w_out_planes, w_out_scales)
-        load_weight_block(nc, w_out_sb, w_out_words, 0)
+        load_weight_block(nc, w_out_sb, w_out_words, 0, BLOCK)
         for m in token_tiles:
             nc.sync.dma_start(out=x_sb[m][:], in_=x[m])
         for col0 in range(BLOCK, D, BLOCK):
-            load_weight_block(nc, w_out_sb, w_out_words, col0)
+            load_weight_block(nc, w_out_sb, w_out_words, col0, BLOCK)
         load_scale_planes(nc, w_fc1_planes, w_fc1_scales)
-        for col0 in range(0, F, BLOCK):
-            load_weight_block(nc, w_fc1_sb, w_fc1_words, col0)
+        for col0 in range(0, F, 2 * BLOCK):
+            load_weight_block(nc, w_fc1_sb, w_fc1_words, col0, 2 * BLOCK)
 
         for m in token_tiles:
             flip_and_quantise(nc, flip_banks, stage, identity, attn_sb[m], attn_codes[m], attn_planes[m])

@@ -22,7 +22,7 @@ BLOCK = 1024
 TILES_PER_BLOCK = BLOCK // N_TILE
 QUADRANT = 32
 EPS = 1e-5
-LAG = 2
+HALF = F // 2
 
 FLOPS = 2 * TOKEN_TILES * P * D * (D + F)
 
@@ -139,8 +139,8 @@ def tile_minitransformerlayer_pb_kernel(
         for col0 in range(BLOCK, D, BLOCK):
             load_weight_block(nc, w_out_sb, w_out_words, col0, BLOCK)
         load_scale_planes(nc, w_fc1_planes, w_fc1_scales)
-        for col0 in range(0, F, 2 * BLOCK):
-            load_weight_block(nc, w_fc1_sb, w_fc1_words, col0, 2 * BLOCK)
+        for col0 in range(0, F, HALF):
+            load_weight_block(nc, w_fc1_sb, w_fc1_words, col0, HALF)
 
         for m in token_tiles:
             flip_and_quantise(nc, flip_banks, stage, identity, attn_sb[m], attn_codes[m], attn_planes[m])
@@ -202,40 +202,35 @@ def tile_minitransformerlayer_pb_kernel(
                         out=std[m][:], in_=sq_sum[m][:], func=ACT.Sqrt, bias=eps[:], scale=1.0 / D
                     )
 
-        blocks = F // BLOCK
-        for step in range(blocks + LAG * (TOKEN_TILES - 1)):
+        for col0 in range(0, F, HALF):
             for m in token_tiles:
-                if step == LAG * m:
+                if col0 == 0:
                     centred = stage.tile([P, D], F32, name="centred")
                     nc.vector.scalar_tensor_tensor(
                         out=centred[:], in0=x_mid[m][:], scalar=neg_mean[m][:], in1=gain,
                         op0=ALU.add, op1=ALU.mult,
                     )
                     nc.vector.reciprocal(out=rstd[m][:], in_=std[m][:])
-                    for col0 in range(0, D, BLOCK):
-                        cols = slice(col0, col0 + BLOCK)
+                    for first in range(0, D, BLOCK):
+                        cols = slice(first, first + BLOCK)
                         nc.vector.scalar_tensor_tensor(
                             out=h_sb[m][:, cols], in0=centred[:, cols], scalar=rstd[m][:], in1=bias[:, cols],
                             op0=ALU.mult, op1=ALU.add,
                         )
                     flip_and_quantise(nc, flip_banks, stage, identity, h_sb[m], h_codes[m], h_planes[m])
-            for m in token_tiles:
-                block = step - LAG * m
-                if 0 <= block < blocks:
-                    col0 = BLOCK * block
-                    products = [
-                        sum_banks.tile([P, N_TILE], F32, name="products", tag="bank")
-                        for c in range(TILES_PER_BLOCK)
-                    ]
-                    for g in range(PASSES):
-                        for c in range(TILES_PER_BLOCK):
-                            mx_pass(
-                                nc, products[c], g, h_codes[m], h_planes[m],
-                                w_fc1_sb, w_fc1_planes, col0 + N_TILE * c,
-                            )
-                    act_sb = results.tile([P, BLOCK], F32, name="act_sb")
-                    for c in range(TILES_PER_BLOCK):
-                        nc.scalar.activation(
-                            out=act_sb[:, N_TILE * c : N_TILE * (c + 1)], in_=products[c][:], func=ACT.Gelu
-                        )
-                    nc.sync.dma_start(out=out_1[m][:, col0 : col0 + BLOCK], in_=act_sb[:])
+                tiles = range(HALF // N_TILE)
+                products = [sum_banks.tile([P, N_TILE], F32, name="products", tag="bank") for c in tiles]
+                if m == 0:
+                    order = [(g, c) for g in range(PASSES) for c in tiles]
+                else:
+                    order = [(g, c) for c in tiles for g in range(PASSES)]
+                for g, c in order:
+                    mx_pass(
+                        nc, products[c], g, h_codes[m], h_planes[m], w_fc1_sb, w_fc1_planes, col0 + N_TILE * c
+                    )
+                act_sb = results.tile([P, HALF], F32, name="act_sb")
+                for c in tiles:
+                    nc.scalar.activation(
+                        out=act_sb[:, N_TILE * c : N_TILE * (c + 1)], in_=products[c][:], func=ACT.Gelu
+                    )
+                nc.sync.dma_start(out=out_1[m][:, col0 : col0 + HALF], in_=act_sb[:])

@@ -89,20 +89,27 @@ def tile_minitransformerlayer_pb_kernel(
     with (
         tc.tile_pool(name="resident", bufs=1) as resident,
         tc.tile_pool(name="stage", bufs=2) as stage,
-        tc.tile_pool(name="results", bufs=4) as results,
         tc.psum_pool(name="flip_banks", bufs=2) as flip_banks,
         tc.psum_pool(name="sum_banks", bufs=6) as sum_banks,
         tc.manual_schedule(),
     ):
         token_tiles = range(TOKEN_TILES)
 
+        attn_in, x_in, x_mid_out = [
+            t.rearrange("b s n -> (b s) n").rearrange("(p m) n -> p m n", m=TOKEN_TILES) for t in (h_attn, x, out_0)
+        ]
+        act_rows = out_1.rearrange("b s n -> (b s) n").rearrange("(p m) n -> p m n", m=TOKEN_TILES)
+        act_out = [act_rows[:, m, :] for m in token_tiles]
+
         w_out_sb = resident.tile([P, PASSES, D], U32, align_bytes=64)
         w_fc1_sb = resident.tile([P, PASSES, F], U32, align_bytes=64)
         w_out_planes = resident.tile([P, D], U8, align_bytes=64)
         w_fc1_planes = resident.tile([P, F], U8, align_bytes=64)
         attn_sb = [resident.tile([P, D], BF16, name="attn_sb%d" % m) for m in token_tiles]
-        x_sb = [resident.tile([P, D], BF16, name="x_sb%d" % m) for m in token_tiles]
-        x_mid = [resident.tile([P, D], F32, name="x_mid%d" % m) for m in token_tiles]
+        x_all = resident.tile([P, TOKEN_TILES, D], BF16)
+        x_mid_all = resident.tile([P, TOKEN_TILES, D], F32)
+        x_sb = [x_all[:, m, :] for m in token_tiles]
+        x_mid = [x_mid_all[:, m, :] for m in token_tiles]
         h_sb = [resident.tile([P, D], BF16, name="h_sb%d" % m) for m in token_tiles]
         attn_codes = [resident.tile([P, D // PACK], U32, name="attn_codes%d" % m, align_bytes=64) for m in token_tiles]
         attn_planes = [resident.tile([P, D // PACK], U8, name="attn_planes%d" % m, align_bytes=64) for m in token_tiles]
@@ -131,11 +138,10 @@ def tile_minitransformerlayer_pb_kernel(
         nc.scalar.dma_start(out=gain_bias_row[0:1, 0:D], in_=g2.rearrange("(o d) -> o d", o=1))
         nc.scalar.dma_start(out=gain_bias_row[0:1, D : 2 * D], in_=b2.rearrange("(o d) -> o d", o=1))
         for m in token_tiles:
-            nc.sync.dma_start(out=attn_sb[m][:], in_=h_attn[m])
+            nc.sync.dma_start(out=attn_sb[m][:], in_=attn_in[:, m, :])
         load_scale_planes(nc, w_out_planes, w_out_scales)
         load_weight_block(nc, w_out_sb, w_out_words, 0, BLOCK)
-        for m in token_tiles:
-            nc.sync.dma_start(out=x_sb[m][:], in_=x[m])
+        nc.sync.dma_start(out=x_all[:], in_=x_in)
         for col0 in range(BLOCK, D, BLOCK):
             load_weight_block(nc, w_out_sb, w_out_words, col0, BLOCK)
         load_scale_planes(nc, w_fc1_planes, w_fc1_scales)
@@ -187,7 +193,6 @@ def tile_minitransformerlayer_pb_kernel(
                         accum_out=row_sums[m][:, first // N_TILE : first // N_TILE + 1],
                     )
                 if last_block:
-                    nc.sync.dma_start(out=out_0[m], in_=x_mid[m][:])
                     total = stage.tile([P, 1], F32, name="total")
                     nc.vector.tensor_reduce(
                         out=total[:], in_=row_sums[m][:], axis=mybir.AxisListType.X, op=ALU.add
@@ -195,42 +200,82 @@ def tile_minitransformerlayer_pb_kernel(
                     nc.vector.tensor_scalar_mul(out=neg_mean[m][:], in0=total[:], scalar1=-1.0 / D)
                     squares = stage.tile([P, D], BF16, name="squares")
                     nc.scalar.activation(
-                        out=squares[:], in_=x_mid[m][:], func=ACT.Square, bias=neg_mean[m][:], scale=1.0,
+                        out=squares[:], in_=x_mid[m], func=ACT.Square, bias=neg_mean[m][:], scale=1.0,
                         accum_out=sq_sum[m][:],
                     )
                     nc.scalar.activation(
                         out=std[m][:], in_=sq_sum[m][:], func=ACT.Sqrt, bias=eps[:], scale=1.0 / D
                     )
 
-        for col0 in range(0, F, HALF):
-            for m in token_tiles:
-                if col0 == 0:
-                    centred = stage.tile([P, D], F32, name="centred")
-                    nc.vector.scalar_tensor_tensor(
-                        out=centred[:], in0=x_mid[m][:], scalar=neg_mean[m][:], in1=gain,
-                        op0=ALU.add, op1=ALU.mult,
-                    )
-                    nc.vector.reciprocal(out=rstd[m][:], in_=std[m][:])
-                    for first in range(0, D, BLOCK):
-                        cols = slice(first, first + BLOCK)
-                        nc.vector.scalar_tensor_tensor(
-                            out=h_sb[m][:, cols], in0=centred[:, cols], scalar=rstd[m][:], in1=bias[:, cols],
-                            op0=ALU.mult, op1=ALU.add,
-                        )
-                    flip_and_quantise(nc, flip_banks, stage, identity, h_sb[m], h_codes[m], h_planes[m])
-                tiles = range(HALF // N_TILE)
-                products = [sum_banks.tile([P, N_TILE], F32, name="products", tag="bank") for c in tiles]
-                if m == 0:
-                    order = [(g, c) for g in range(PASSES) for c in tiles]
-                else:
-                    order = [(g, c) for c in tiles for g in range(PASSES)]
-                for g, c in order:
-                    mx_pass(
-                        nc, products[c], g, h_codes[m], h_planes[m], w_fc1_sb, w_fc1_planes, col0 + N_TILE * c
-                    )
-                act_sb = results.tile([P, HALF], F32, name="act_sb")
-                for c in tiles:
-                    nc.scalar.activation(
-                        out=act_sb[:, N_TILE * c : N_TILE * (c + 1)], in_=products[c][:], func=ACT.Gelu
-                    )
-                nc.sync.dma_start(out=out_1[m][:, col0 : col0 + HALF], in_=act_sb[:])
+        nc.sync.dma_start(out=x_mid_out, in_=x_mid_all[:])
+
+        def layer_norm(m):
+            centred = stage.tile([P, D], F32, name="centred")
+            nc.vector.scalar_tensor_tensor(
+                out=centred[:], in0=x_mid[m], scalar=neg_mean[m][:], in1=gain,
+                op0=ALU.add, op1=ALU.mult,
+            )
+            nc.vector.reciprocal(out=rstd[m][:], in_=std[m][:])
+            for first in range(0, D, BLOCK):
+                cols = slice(first, first + BLOCK)
+                nc.vector.scalar_tensor_tensor(
+                    out=h_sb[m][:, cols], in0=centred[:, cols], scalar=rstd[m][:], in1=bias[:, cols],
+                    op0=ALU.mult, op1=ALU.add,
+                )
+            flip_and_quantise(nc, flip_banks, stage, identity, h_sb[m], h_codes[m], h_planes[m])
+
+        tiles = range(HALF // N_TILE)
+        products = {}
+
+        def act_pass(m, half, g, c):
+            if g == 0:
+                products[m, half, c] = sum_banks.tile([P, N_TILE], F32, name="products", tag="bank")
+            mx_pass(
+                nc, products[m, half, c], g, h_codes[m], h_planes[m],
+                w_fc1_sb, w_fc1_planes, HALF * half + N_TILE * c,
+            )
+
+        act_sb = {
+            (m, half): resident.tile([P, HALF], F32, name="act_sb%d%d" % (m, half))
+            for m in token_tiles
+            for half in range(F // HALF)
+        }
+
+        def gelu(m, half, c):
+            nc.scalar.activation(
+                out=act_sb[m, half][:, N_TILE * c : N_TILE * (c + 1)], in_=products[m, half, c][:], func=ACT.Gelu
+            )
+
+        def store(m, half, first, last):
+            cols = slice(N_TILE * first, N_TILE * (last + 1))
+            out_cols = slice(HALF * half + N_TILE * first, HALF * half + N_TILE * (last + 1))
+            nc.sync.dma_start(out=act_out[m][:, out_cols], in_=act_sb[m, half][:, cols])
+
+        layer_norm(0)
+        for g in range(PASSES):
+            for c in tiles:
+                act_pass(0, 0, g, c)
+        for c in tiles:
+            gelu(0, 0, c)
+        store(0, 0, 0, 3)
+        for g in range(2):
+            for c in tiles:
+                act_pass(0, 1, g, c)
+        layer_norm(1)
+        for c in tiles:
+            for g in range(PASSES):
+                act_pass(1, 0, g, c)
+            gelu(1, 0, c)
+        store(1, 0, 0, 3)
+        for g in range(2, PASSES):
+            for c in tiles:
+                act_pass(0, 1, g, c)
+        for c in tiles:
+            gelu(0, 1, c)
+        store(0, 1, 0, 3)
+        for c in tiles:
+            for g in range(PASSES):
+                act_pass(1, 1, g, c)
+            gelu(1, 1, c)
+            if c > 0:
+                store(1, 1, 0 if c == 1 else c, c)

@@ -36,36 +36,38 @@ def load_scale_planes(nc, planes, scales):
         )
 
 
-def load_weight_block(nc, w_sb, words, col0, width):
-    for g in range(PASSES):
-        rows = words[g].rearrange("p n t -> p (n t)")
-        nc.sync.dma_start(
-            out=w_sb[:, g, col0 : col0 + width].bitcast(I32),
-            in_=rows[:, PACK * col0 : PACK * (col0 + width)].bitcast(I32),
-        )
+def load_weights(nc, w_sb, words, g, col0, width):
+    rows = words[g].rearrange("p n t -> p (n t)")
+    nc.sync.dma_start(
+        out=w_sb[:, g, col0 : col0 + width].bitcast(I32),
+        in_=rows[:, PACK * col0 : PACK * (col0 + width)].bitcast(I32),
+    )
 
 
-def flip_and_quantise(nc, flip_banks, stage, identity, src, codes, planes):
+def flip(nc, flip_banks, stage, identity, src, half):
     pairs = src[:].bitcast(F32)
     pairs_per_pass = K_PASS // 2
-    for half in range(PASSES // 2):
-        flipped = flip_banks.tile([P, 2, 2, P], F32, name="flipped")
-        for i in range(2):
-            g = 2 * half + i
-            for u in range(2):
-                nc.tensor.transpose(
-                    flipped[:, i, u, :],
-                    pairs[:, pairs_per_pass * g + u : pairs_per_pass * (g + 1) : 2],
-                    identity[:],
-                )
-        grouped = stage.tile([P, 2, P, PACK], BF16, name="grouped", align_bytes=64)
-        nc.scalar.copy(out=grouped[:].bitcast(F32), in_=flipped[:].rearrange("p g u r -> p g r u"))
-        cols = slice(2 * P * half, 2 * P * (half + 1))
-        nc.vector.quantize_mx(
-            out=codes[:, cols].bitcast(FP8X4),
-            scales=planes[:, cols],
-            in_=grouped[:].rearrange("p g r t -> p (g r t)"),
-        )
+    flipped = flip_banks.tile([P, 2, 2, P], F32, name="flipped")
+    for i in range(2):
+        g = 2 * half + i
+        for u in range(2):
+            nc.tensor.transpose(
+                flipped[:, i, u, :],
+                pairs[:, pairs_per_pass * g + u : pairs_per_pass * (g + 1) : 2],
+                identity[:],
+            )
+    grouped = stage.tile([P, 2, P, PACK], BF16, name="grouped", align_bytes=64)
+    nc.scalar.copy(out=grouped[:].bitcast(F32), in_=flipped[:].rearrange("p g u r -> p g r u"))
+    return grouped
+
+
+def quantise(nc, grouped, codes, planes, half):
+    cols = slice(2 * P * half, 2 * P * (half + 1))
+    nc.vector.quantize_mx(
+        out=codes[:, cols].bitcast(FP8X4),
+        scales=planes[:, cols],
+        in_=grouped[:].rearrange("p g r t -> p (g r t)"),
+    )
 
 
 def mx_pass(nc, sums, g, codes, planes, w_sb, w_planes, col0):
@@ -117,11 +119,15 @@ def tile_minitransformerlayer_pb_kernel(
         h_planes = [resident.tile([P, D // PACK], U8, name="h_planes%d" % m, align_bytes=64) for m in token_tiles]
         row_sums = [resident.tile([P, D // N_TILE], F32, name="row_sums%d" % m) for m in token_tiles]
         neg_mean = [resident.tile([P, 1], F32, name="neg_mean%d" % m) for m in token_tiles]
-        sq_sum = [resident.tile([P, 1], F32, name="sq_sum%d" % m) for m in token_tiles]
+        neg_shift = [resident.tile([P, 1], F32, name="neg_shift%d" % m) for m in token_tiles]
+        sq_sums = [resident.tile([P, D // N_TILE], F32, name="sq_sums%d" % m) for m in token_tiles]
+        var_part = [resident.tile([P, 1], F32, name="var_part%d" % m) for m in token_tiles]
+        var_rest = [resident.tile([P, 1], F32, name="var_rest%d" % m) for m in token_tiles]
+        shift_sq = [resident.tile([P, 1], F32, name="shift_sq%d" % m) for m in token_tiles]
         std = [resident.tile([P, 1], F32, name="std%d" % m) for m in token_tiles]
         rstd = [resident.tile([P, 1], F32, name="rstd%d" % m) for m in token_tiles]
         gain_bias_row = resident.tile([P, 2 * D], BF16)
-        gain_bias = resident.tile([P, 2 * D], BF16)
+        gain = resident.tile([P, D], BF16)
         ones = resident.tile([P, P], BF16)
         identity = resident.tile([P, P], F32)
         eps = resident.tile([P, 1], F32)
@@ -140,89 +146,157 @@ def tile_minitransformerlayer_pb_kernel(
         for m in token_tiles:
             nc.sync.dma_start(out=attn_sb[m][:], in_=attn_in[:, m, :])
         load_scale_planes(nc, w_out_planes, w_out_scales)
-        load_weight_block(nc, w_out_sb, w_out_words, 0, BLOCK)
+        for g in range(PASSES):
+            load_weights(nc, w_out_sb, w_out_words, g, 0, BLOCK)
         nc.sync.dma_start(out=x_all[:], in_=x_in)
-        for col0 in range(BLOCK, D, BLOCK):
-            load_weight_block(nc, w_out_sb, w_out_words, col0, BLOCK)
+        for g in range(PASSES - 1):
+            load_weights(nc, w_out_sb, w_out_words, g, BLOCK, BLOCK)
+        for col0 in range(BLOCK, D, N_TILE):
+            load_weights(nc, w_out_sb, w_out_words, PASSES - 1, col0, N_TILE)
         load_scale_planes(nc, w_fc1_planes, w_fc1_scales)
         for col0 in range(0, F, HALF):
-            load_weight_block(nc, w_fc1_sb, w_fc1_words, col0, HALF)
+            for g in range(PASSES):
+                load_weights(nc, w_fc1_sb, w_fc1_words, g, col0, HALF)
 
         for m in token_tiles:
-            flip_and_quantise(nc, flip_banks, stage, identity, attn_sb[m], attn_codes[m], attn_planes[m])
+            for half in range(PASSES // 2):
+                grouped = flip(nc, flip_banks, stage, identity, attn_sb[m], half)
+                quantise(nc, grouped, attn_codes[m], attn_planes[m], half)
 
-        for col0 in range(0, 2 * D, 2 * N_TILE):
-            spread = sum_banks.tile([P, 2 * N_TILE], BF16, name="spread", tag="bank")
+        sums = {}
+
+        def out_pass(m, tile, g):
+            if g == 0:
+                sums[m, tile] = sum_banks.tile([P, N_TILE], F32, name="sums", tag="bank")
+            mx_pass(nc, sums[m, tile], g, attn_codes[m], attn_planes[m], w_out_sb, w_out_planes, N_TILE * tile)
+
+        def residual_add(m, tile):
+            cols = slice(N_TILE * tile, N_TILE * (tile + 1))
+            nc.vector.scalar_tensor_tensor(
+                out=x_mid[m][:, cols], in0=sums[m, tile][:], scalar=1.0, in1=x_sb[m][:, cols],
+                op0=ALU.mult, op1=ALU.add, accum_out=row_sums[m][:, tile : tile + 1],
+            )
+
+        def minus_shift(m):
+            nc.vector.tensor_scalar_mul(out=neg_shift[m][:], in0=row_sums[m][:, 0:1], scalar1=-1.0 / N_TILE)
+
+        def squares(m, tile):
+            squared = stage.tile([P, N_TILE], BF16, name="squared")
+            nc.scalar.activation(
+                out=squared[:], in_=x_mid[m][:, N_TILE * tile : N_TILE * (tile + 1)], func=ACT.Square,
+                bias=neg_shift[m][:], scale=1.0, accum_out=sq_sums[m][:, tile : tile + 1],
+            )
+
+        def first_squares(m):
+            scaled = stage.tile([P, D // N_TILE], F32, name="scaled")
+            nc.vector.tensor_scalar(
+                out=scaled[:, 0:3], in0=sq_sums[m][:, 0:3], scalar1=1.0 / D, scalar2=EPS,
+                op0=ALU.mult, op1=ALU.add, accum_out=var_part[m][:],
+            )
+
+        def minus_mean(m):
+            scaled = stage.tile([P, D // N_TILE], F32, name="scaled")
+            nc.vector.tensor_scalar(
+                out=scaled[:], in0=row_sums[m][:], scalar1=-1.0 / D, scalar2=None,
+                op0=ALU.mult, op1=ALU.add, accum_out=neg_mean[m][:],
+            )
+
+        def deviation(m):
+            nc.scalar.activation(
+                out=shift_sq[m][:], in_=neg_shift[m][:], func=ACT.Square, bias=neg_mean[m][:], scale=-1.0
+            )
+            nc.scalar.activation(
+                out=var_rest[m][:], in_=shift_sq[m][:], func=ACT.Identity, bias=var_part[m][:], scale=-1.0
+            )
+            nc.scalar.activation(
+                out=std[m][:], in_=sq_sums[m][:, 3:4], func=ACT.Sqrt, bias=var_rest[m][:], scale=1.0 / D
+            )
+
+        for g in range(PASSES):
+            for m in token_tiles:
+                for tile in (0, 1):
+                    out_pass(m, tile, g)
+
+        def spread(pool, tag, col0):
+            bank = pool.tile([P, 2 * N_TILE], BF16, name="spread", tag=tag)
             for i in range(2):
                 cols = slice(col0 + N_TILE * i, col0 + N_TILE * (i + 1))
                 nc.tensor.matmul(
-                    out=spread[:, N_TILE * i : N_TILE * (i + 1)],
+                    out=bank[:, N_TILE * i : N_TILE * (i + 1)],
                     lhsT=ones[:],
                     rhs=gain_bias_row[:, cols],
                     start=True,
                     stop=True,
                 )
-            nc.scalar.copy(out=gain_bias[:, col0 : col0 + 2 * N_TILE], in_=spread[:])
-        gain = gain_bias[:, 0:D]
-        bias = gain_bias[:, D : 2 * D]
+            return bank
 
         for col0 in range(0, D, BLOCK):
-            sums = [
-                [sum_banks.tile([P, N_TILE], F32, name="sums", tag="bank") for c in range(TILES_PER_BLOCK)]
-                for m in token_tiles
-            ]
-            for g in range(PASSES):
-                for m in token_tiles:
-                    for c in range(TILES_PER_BLOCK):
-                        mx_pass(
-                            nc, sums[m][c], g, attn_codes[m], attn_planes[m],
-                            w_out_sb, w_out_planes, col0 + N_TILE * c,
-                        )
-            last_block = col0 + BLOCK == D
+            bank = spread(flip_banks, "flipped", col0)
+            nc.scalar.copy(out=gain[:, col0 : col0 + BLOCK], in_=bank[:])
+
+        for tile in (0, 1):
             for m in token_tiles:
-                for c in range(TILES_PER_BLOCK):
-                    first = col0 + N_TILE * c
-                    cols = slice(first, first + N_TILE)
-                    nc.vector.scalar_tensor_tensor(
-                        out=x_mid[m][:, cols],
-                        in0=sums[m][c][:],
-                        scalar=1.0,
-                        in1=x_sb[m][:, cols],
-                        op0=ALU.mult,
-                        op1=ALU.add,
-                        accum_out=row_sums[m][:, first // N_TILE : first // N_TILE + 1],
-                    )
-                if last_block:
-                    total = stage.tile([P, 1], F32, name="total")
-                    nc.vector.tensor_reduce(
-                        out=total[:], in_=row_sums[m][:], axis=mybir.AxisListType.X, op=ALU.add
-                    )
-                    nc.vector.tensor_scalar_mul(out=neg_mean[m][:], in0=total[:], scalar1=-1.0 / D)
-                    squares = stage.tile([P, D], BF16, name="squares")
-                    nc.scalar.activation(
-                        out=squares[:], in_=x_mid[m], func=ACT.Square, bias=neg_mean[m][:], scale=1.0,
-                        accum_out=sq_sum[m][:],
-                    )
-                    nc.scalar.activation(
-                        out=std[m][:], in_=sq_sum[m][:], func=ACT.Sqrt, bias=eps[:], scale=1.0 / D
-                    )
+                residual_add(m, tile)
+            for m in token_tiles:
+                if tile == 0:
+                    minus_shift(m)
+                squares(m, tile)
 
-        nc.sync.dma_start(out=x_mid_out, in_=x_mid_all[:])
+        for g in range(PASSES - 1):
+            for m in token_tiles:
+                for tile in (2, 3):
+                    out_pass(m, tile, g)
+        for tile in (2, 3):
+            for m in token_tiles:
+                out_pass(m, tile, PASSES - 1)
+        bias = [spread(sum_banks, "bank", D + col0) for col0 in range(0, D, BLOCK)]
 
-        def layer_norm(m):
-            centred = stage.tile([P, D], F32, name="centred")
+        centred = [stage.tile([P, D], F32, name="centred") for m in token_tiles]
+
+        def centre(m, col0, width):
+            cols = slice(col0, col0 + width)
             nc.vector.scalar_tensor_tensor(
-                out=centred[:], in0=x_mid[m], scalar=neg_mean[m][:], in1=gain,
+                out=centred[m][:, cols], in0=x_mid[m][:, cols], scalar=neg_mean[m][:], in1=gain[:, cols],
                 op0=ALU.add, op1=ALU.mult,
             )
-            nc.vector.reciprocal(out=rstd[m][:], in_=std[m][:])
-            for first in range(0, D, BLOCK):
-                cols = slice(first, first + BLOCK)
-                nc.vector.scalar_tensor_tensor(
-                    out=h_sb[m][:, cols], in0=centred[:, cols], scalar=rstd[m][:], in1=bias[:, cols],
-                    op0=ALU.mult, op1=ALU.add,
-                )
-            flip_and_quantise(nc, flip_banks, stage, identity, h_sb[m], h_codes[m], h_planes[m])
+
+        def normalise(m, half):
+            cols = slice(BLOCK * half, BLOCK * (half + 1))
+            nc.vector.scalar_tensor_tensor(
+                out=h_sb[m][:, cols], in0=centred[m][:, cols], scalar=rstd[m][:], in1=bias[half][:],
+                op0=ALU.mult, op1=ALU.add,
+            )
+
+        residual_add(0, 2)
+        residual_add(1, 2)
+        squares(0, 2)
+        squares(1, 2)
+        residual_add(0, 3)
+        squares(0, 3)
+        first_squares(0)
+        minus_mean(0)
+        deviation(0)
+        first_squares(1)
+        centre(0, 0, BLOCK)
+        centre(0, BLOCK, N_TILE)
+        nc.vector.reciprocal(out=rstd[0][:], in_=std[0][:])
+        centre(0, BLOCK + N_TILE, N_TILE)
+        normalise(0, 0)
+        grouped_0 = flip(nc, flip_banks, stage, identity, h_sb[0], 0)
+        normalise(0, 1)
+        grouped_1 = flip(nc, flip_banks, stage, identity, h_sb[0], 1)
+        residual_add(1, 3)
+        squares(1, 3)
+        nc.sync.dma_start(out=x_mid_out, in_=x_mid_all[:])
+        quantise(nc, grouped_0, h_codes[0], h_planes[0], 0)
+        minus_mean(1)
+        deviation(1)
+        nc.scalar.activation(out=warm[:], in_=eps[:], func=ACT.Gelu)
+        centre(1, 0, N_TILE)
+        quantise(nc, grouped_1, h_codes[0], h_planes[0], 1)
+        centre(1, N_TILE, N_TILE)
+        nc.vector.reciprocal(out=rstd[1][:], in_=std[1][:])
+        centre(1, BLOCK, BLOCK)
 
         tiles = range(HALF // N_TILE)
         products = {}
@@ -251,31 +325,37 @@ def tile_minitransformerlayer_pb_kernel(
             out_cols = slice(HALF * half + N_TILE * first, HALF * half + N_TILE * (last + 1))
             nc.sync.dma_start(out=act_out[m][:, out_cols], in_=act_sb[m, half][:, cols])
 
-        layer_norm(0)
+        pairs = ((0, 1), (2, 3))
         for g in range(PASSES):
             for c in tiles:
                 act_pass(0, 0, g, c)
+        normalise(1, 0)
+        grouped_0 = flip(nc, flip_banks, stage, identity, h_sb[1], 0)
+        normalise(1, 1)
+        grouped_1 = flip(nc, flip_banks, stage, identity, h_sb[1], 1)
+        quantise(nc, grouped_0, h_codes[1], h_planes[1], 0)
+        quantise(nc, grouped_1, h_codes[1], h_planes[1], 1)
         for c in tiles:
             gelu(0, 0, c)
         store(0, 0, 0, 3)
-        for g in range(2):
-            for c in tiles:
-                act_pass(0, 1, g, c)
-        layer_norm(1)
-        for c in tiles:
+        for pair in pairs:
             for g in range(PASSES):
-                act_pass(1, 0, g, c)
-            gelu(1, 0, c)
+                for c in pair:
+                    act_pass(1, 0, g, c)
+            for c in pair:
+                gelu(1, 0, c)
         store(1, 0, 0, 3)
-        for g in range(2, PASSES):
+        for g in range(PASSES):
             for c in tiles:
                 act_pass(0, 1, g, c)
         for c in tiles:
             gelu(0, 1, c)
         store(0, 1, 0, 3)
-        for c in tiles:
+        for pair in pairs:
             for g in range(PASSES):
-                act_pass(1, 1, g, c)
-            gelu(1, 1, c)
-            if c > 0:
-                store(1, 1, 0 if c == 1 else c, c)
+                for c in pair:
+                    act_pass(1, 1, g, c)
+            for c in pair:
+                gelu(1, 1, c)
+                if c != 0:
+                    store(1, 1, 0 if c == 1 else c, c)

@@ -44,18 +44,26 @@ def load_weights(nc, w_sb, words, g, col0, width):
     )
 
 
-def flip(nc, flip_banks, stage, identity, src, half):
+def by_word_half(ap):
+    return ap.rearrange("n (p u e) -> n u p e", u=2, e=2)
+
+
+def in_order(ap):
+    return ap.rearrange("n (u p e) -> n u p e", u=2, e=2)
+
+
+def flip(nc, flip_banks, stage, identity, src, half, split):
     pairs = src[:].bitcast(F32)
     pairs_per_pass = K_PASS // 2
     flipped = flip_banks.tile([P, 2, 2, P], F32, name="flipped")
     for i in range(2):
         g = 2 * half + i
         for u in range(2):
-            nc.tensor.transpose(
-                flipped[:, i, u, :],
-                pairs[:, pairs_per_pass * g + u : pairs_per_pass * (g + 1) : 2],
-                identity[:],
-            )
+            if split:
+                words = pairs[:, pairs_per_pass * g + P * u : pairs_per_pass * g + P * (u + 1)]
+            else:
+                words = pairs[:, pairs_per_pass * g + u : pairs_per_pass * (g + 1) : 2]
+            nc.tensor.transpose(flipped[:, i, u, :], words, identity[:])
     grouped = stage.tile([P, 2, P, PACK], BF16, name="grouped", align_bytes=64)
     nc.scalar.copy(out=grouped[:].bitcast(F32), in_=flipped[:].rearrange("p g u r -> p g r u"))
     return grouped
@@ -128,15 +136,15 @@ def tile_minitransformerlayer_pb_kernel(
         rstd = [resident.tile([P, 1], F32, name="rstd%d" % m) for m in token_tiles]
         gain_bias_row = resident.tile([P, 2 * D], BF16)
         gain = resident.tile([P, D], BF16)
-        ones = resident.tile([P, P], BF16)
+        ones = resident.tile([P, N_TILE], BF16)
         identity = resident.tile([P, P], F32)
         eps = resident.tile([P, 1], F32)
         warm = resident.tile([P, 1], F32)
 
+        nc.vector.memset(ones[:], 1.0)
         nc.vector.memset(eps[:], EPS)
         nc.vector.memset(w_out_planes[:].bitcast(I32), 0)
         nc.vector.memset(gain_bias_row[:].bitcast(I32), 0)
-        nc.vector.memset(ones[:], 1.0)
         nc.vector.memset(w_fc1_planes[:].bitcast(I32), 0)
         make_identity(nc, identity[:])
         nc.scalar.activation(out=warm[:], in_=eps[:], func=ACT.Sqrt)
@@ -158,9 +166,16 @@ def tile_minitransformerlayer_pb_kernel(
             for g in range(PASSES):
                 load_weights(nc, w_fc1_sb, w_fc1_words, g, col0, HALF)
 
+        def keep_warm(n):
+            unread = flip_banks.tile([P, N_TILE], F32, name="unread", tag="flipped")
+            for i in range(n):
+                nc.tensor.matmul(out=unread[:], lhsT=ones[:, 0:P], rhs=ones[:], start=True, stop=True)
+
+        keep_warm(4)
+
         for m in token_tiles:
             for half in range(PASSES // 2):
-                grouped = flip(nc, flip_banks, stage, identity, attn_sb[m], half)
+                grouped = flip(nc, flip_banks, stage, identity, attn_sb[m], half, False)
                 quantise(nc, grouped, attn_codes[m], attn_planes[m], half)
 
         sums = {}
@@ -222,9 +237,9 @@ def tile_minitransformerlayer_pb_kernel(
             for i in range(2):
                 cols = slice(col0 + N_TILE * i, col0 + N_TILE * (i + 1))
                 nc.tensor.matmul(
-                    out=bank[:, N_TILE * i : N_TILE * (i + 1)],
-                    lhsT=ones[:],
-                    rhs=gain_bias_row[:, cols],
+                    out=in_order(bank[:, N_TILE * i : N_TILE * (i + 1)]),
+                    lhsT=ones[:, 0:P],
+                    rhs=by_word_half(gain_bias_row[:, cols]),
                     start=True,
                     stop=True,
                 )
@@ -250,14 +265,18 @@ def tile_minitransformerlayer_pb_kernel(
             for m in token_tiles:
                 out_pass(m, tile, PASSES - 1)
         bias = [spread(sum_banks, "bank", D + col0) for col0 in range(0, D, BLOCK)]
+        keep_warm(8)
 
         centred = [stage.tile([P, D], F32, name="centred") for m in token_tiles]
 
-        def centre(m, col0, width):
-            cols = slice(col0, col0 + width)
+        def centre(m, half, u):
+            cols = slice(BLOCK * half, BLOCK * (half + 1))
+            natural = x_mid[m][:, cols].rearrange("n (g p u e) -> n u g p e", g=2, u=2, e=2)[:, u]
+            split = [
+                t[:, cols].rearrange("n (g u p e) -> n u g p e", g=2, u=2, e=2)[:, u] for t in (centred[m], gain)
+            ]
             nc.vector.scalar_tensor_tensor(
-                out=centred[m][:, cols], in0=x_mid[m][:, cols], scalar=neg_mean[m][:], in1=gain[:, cols],
-                op0=ALU.add, op1=ALU.mult,
+                out=split[0], in0=natural, scalar=neg_mean[m][:], in1=split[1], op0=ALU.add, op1=ALU.mult
             )
 
         def normalise(m, half):
@@ -277,14 +296,16 @@ def tile_minitransformerlayer_pb_kernel(
         minus_mean(0)
         deviation(0)
         first_squares(1)
-        centre(0, 0, BLOCK)
-        centre(0, BLOCK, N_TILE)
+        centre(0, 0, 0)
+        centre(0, 0, 1)
+        centre(0, 1, 0)
         nc.vector.reciprocal(out=rstd[0][:], in_=std[0][:])
-        centre(0, BLOCK + N_TILE, N_TILE)
+        centre(0, 1, 1)
         normalise(0, 0)
-        grouped_0 = flip(nc, flip_banks, stage, identity, h_sb[0], 0)
+        grouped_0 = flip(nc, flip_banks, stage, identity, h_sb[0], 0, True)
+        keep_warm(2)
         normalise(0, 1)
-        grouped_1 = flip(nc, flip_banks, stage, identity, h_sb[0], 1)
+        grouped_1 = flip(nc, flip_banks, stage, identity, h_sb[0], 1, True)
         residual_add(1, 3)
         squares(1, 3)
         nc.sync.dma_start(out=x_mid_out, in_=x_mid_all[:])
@@ -292,11 +313,12 @@ def tile_minitransformerlayer_pb_kernel(
         minus_mean(1)
         deviation(1)
         nc.scalar.activation(out=warm[:], in_=eps[:], func=ACT.Gelu)
-        centre(1, 0, N_TILE)
+        centre(1, 0, 0)
         quantise(nc, grouped_1, h_codes[0], h_planes[0], 1)
-        centre(1, N_TILE, N_TILE)
+        centre(1, 0, 1)
         nc.vector.reciprocal(out=rstd[1][:], in_=std[1][:])
-        centre(1, BLOCK, BLOCK)
+        centre(1, 1, 0)
+        centre(1, 1, 1)
 
         tiles = range(HALF // N_TILE)
         products = {}
@@ -329,15 +351,19 @@ def tile_minitransformerlayer_pb_kernel(
         for g in range(PASSES):
             for c in tiles:
                 act_pass(0, 0, g, c)
+        gelu(0, 0, 0)
+        gelu(0, 0, 1)
         normalise(1, 0)
-        grouped_0 = flip(nc, flip_banks, stage, identity, h_sb[1], 0)
+        grouped_0 = flip(nc, flip_banks, stage, identity, h_sb[1], 0, True)
+        gelu(0, 0, 2)
         normalise(1, 1)
-        grouped_1 = flip(nc, flip_banks, stage, identity, h_sb[1], 1)
+        grouped_1 = flip(nc, flip_banks, stage, identity, h_sb[1], 1, True)
+        gelu(0, 0, 3)
+        store(0, 0, 0, 3)
         quantise(nc, grouped_0, h_codes[1], h_planes[1], 0)
         quantise(nc, grouped_1, h_codes[1], h_planes[1], 1)
-        for c in tiles:
-            gelu(0, 0, c)
-        store(0, 0, 0, 3)
+        for c in (0, 1):
+            act_pass(0, 1, 0, c)
         for pair in pairs:
             for g in range(PASSES):
                 for c in pair:
@@ -347,7 +373,8 @@ def tile_minitransformerlayer_pb_kernel(
         store(1, 0, 0, 3)
         for g in range(PASSES):
             for c in tiles:
-                act_pass(0, 1, g, c)
+                if g > 0 or c > 1:
+                    act_pass(0, 1, g, c)
         for c in tiles:
             gelu(0, 1, c)
         store(0, 1, 0, 3)

@@ -345,7 +345,8 @@ def tile_minitransformerlayer_pb_kernel(
         def store(m, half, first, last):
             cols = slice(N_TILE * first, N_TILE * (last + 1))
             out_cols = slice(HALF * half + N_TILE * first, HALF * half + N_TILE * (last + 1))
-            nc.sync.dma_start(out=act_out[m][:, out_cols], in_=act_sb[m, half][:, cols])
+            queue = nc.scalar if m + half == 1 else nc.sync
+            queue.dma_start(out=act_out[m][:, out_cols], in_=act_sb[m, half][:, cols])
 
         pairs = ((0, 1), (2, 3))
         for g in range(PASSES):

import concourse.mybir as mybir
from concourse.masks import make_identity

BF16 = mybir.dt.bfloat16
F32 = mybir.dt.float32
I32 = mybir.dt.int32
U32 = mybir.dt.uint32
U8 = mybir.dt.uint8
FP8X4 = mybir.dt.float8_e4m3fn_x4
ALU = mybir.AluOpType
ACT = mybir.ActivationFunctionType

P = 128
PACK = 4
K_PASS = P * PACK
TOKEN_TILES = 2
D = 2048
F = 4096
PASSES = D // K_PASS
N_TILE = 512
BLOCK = 1024
TILES_PER_BLOCK = BLOCK // N_TILE
QUADRANT = 32
EPS = 1e-5
HALF = F // 2

FLOPS = 2 * TOKEN_TILES * P * D * (D + F)


def load_scale_planes(nc, planes, scales):
    for quadrant in range(P // QUADRANT):
        first = QUADRANT * quadrant
        nc.sync.dma_start(
            out=planes[first : first + PACK * PASSES, :].bitcast(I32),
            in_=scales[:, PACK * quadrant : PACK * (quadrant + 1), :].bitcast(I32),
        )


def load_weights(nc, w_sb, words, g, col0, width):
    rows = words[g].rearrange("p n t -> p (n t)")
    nc.sync.dma_start(
        out=w_sb[:, g, col0 : col0 + width].bitcast(I32),
        in_=rows[:, PACK * col0 : PACK * (col0 + width)].bitcast(I32),
    )


def by_word_half(ap):
    return ap.rearrange("n (p u e) -> n u p e", u=2, e=2)


def in_order(ap):
    return ap.rearrange("n (u p e) -> n u p e", u=2, e=2)


def flip(nc, flip_banks, stage, identity, src, half, split):
    pairs = src[:].bitcast(F32)
    pairs_per_pass = K_PASS // 2
    flipped = flip_banks.tile([P, 2, 2, P], F32, name="flipped")
    for i in range(2):
        g = 2 * half + i
        for u in range(2):
            if split:
                words = pairs[:, pairs_per_pass * g + P * u : pairs_per_pass * g + P * (u + 1)]
            else:
                words = pairs[:, pairs_per_pass * g + u : pairs_per_pass * (g + 1) : 2]
            nc.tensor.transpose(flipped[:, i, u, :], words, identity[:])
    grouped = stage.tile([P, 2, P, PACK], BF16, name="grouped", align_bytes=64)
    nc.scalar.copy(out=grouped[:].bitcast(F32), in_=flipped[:].rearrange("p g u r -> p g r u"))
    return grouped


def quantise(nc, grouped, codes, planes, half):
    cols = slice(2 * P * half, 2 * P * (half + 1))
    nc.vector.quantize_mx(
        out=codes[:, cols].bitcast(FP8X4),
        scales=planes[:, cols],
        in_=grouped[:].rearrange("p g r t -> p (g r t)"),
    )


def mx_pass(nc, sums, g, codes, planes, w_sb, w_planes, col0):
    tokens = slice(P * g, P * (g + 1))
    cols = slice(col0, col0 + N_TILE)
    nc.tensor.matmul_mx(
        out=sums[:],
        lhsT=codes[:, tokens].bitcast(FP8X4),
        lhsT_scale=planes[:, tokens],
        rhs=w_sb[:, g, cols].bitcast(FP8X4),
        rhs_scale=w_planes[PACK * g : P, cols],
        start=(g == 0),
        stop=(g == PASSES - 1),
    )


def tile_minitransformerlayer_pb_kernel(
    tc, h_attn, x, w_out_words, w_out_scales, w_fc1_words, w_fc1_scales, g2, b2, out_0, out_1
):
    nc = tc.nc
    with (
        tc.tile_pool(name="resident", bufs=1) as resident,
        tc.tile_pool(name="stage", bufs=2) as stage,
        tc.psum_pool(name="flip_banks", bufs=2) as flip_banks,
        tc.psum_pool(name="sum_banks", bufs=6) as sum_banks,
        tc.manual_schedule(),
    ):
        token_tiles = range(TOKEN_TILES)

        attn_in, x_in, x_mid_out = [
            t.rearrange("b s n -> (b s) n").rearrange("(p m) n -> p m n", m=TOKEN_TILES) for t in (h_attn, x, out_0)
        ]
        act_rows = out_1.rearrange("b s n -> (b s) n").rearrange("(p m) n -> p m n", m=TOKEN_TILES)
        act_out = [act_rows[:, m, :] for m in token_tiles]

        w_out_sb = resident.tile([P, PASSES, D], U32, align_bytes=64)
        w_fc1_sb = resident.tile([P, PASSES, F], U32, align_bytes=64)
        w_out_planes = resident.tile([P, D], U8, align_bytes=64)
        w_fc1_planes = resident.tile([P, F], U8, align_bytes=64)
        attn_sb = [resident.tile([P, D], BF16, name="attn_sb%d" % m) for m in token_tiles]
        x_all = resident.tile([P, TOKEN_TILES, D], BF16)
        x_mid_all = resident.tile([P, TOKEN_TILES, D], F32)
        x_sb = [x_all[:, m, :] for m in token_tiles]
        x_mid = [x_mid_all[:, m, :] for m in token_tiles]
        h_sb = [resident.tile([P, D], BF16, name="h_sb%d" % m) for m in token_tiles]
        attn_codes = [resident.tile([P, D // PACK], U32, name="attn_codes%d" % m, align_bytes=64) for m in token_tiles]
        attn_planes = [resident.tile([P, D // PACK], U8, name="attn_planes%d" % m, align_bytes=64) for m in token_tiles]
        h_codes = [resident.tile([P, D // PACK], U32, name="h_codes%d" % m, align_bytes=64) for m in token_tiles]
        h_planes = [resident.tile([P, D // PACK], U8, name="h_planes%d" % m, align_bytes=64) for m in token_tiles]
        row_sums = [resident.tile([P, D // N_TILE], F32, name="row_sums%d" % m) for m in token_tiles]
        neg_mean = [resident.tile([P, 1], F32, name="neg_mean%d" % m) for m in token_tiles]
        neg_shift = [resident.tile([P, 1], F32, name="neg_shift%d" % m) for m in token_tiles]
        sq_sums = [resident.tile([P, D // N_TILE], F32, name="sq_sums%d" % m) for m in token_tiles]
        var_part = [resident.tile([P, 1], F32, name="var_part%d" % m) for m in token_tiles]
        var_rest = [resident.tile([P, 1], F32, name="var_rest%d" % m) for m in token_tiles]
        shift_sq = [resident.tile([P, 1], F32, name="shift_sq%d" % m) for m in token_tiles]
        std = [resident.tile([P, 1], F32, name="std%d" % m) for m in token_tiles]
        rstd = [resident.tile([P, 1], F32, name="rstd%d" % m) for m in token_tiles]
        gain_bias_row = resident.tile([P, 2 * D], BF16)
        gain = resident.tile([P, D], BF16)
        ones = resident.tile([P, N_TILE], BF16)
        identity = resident.tile([P, P], F32)
        eps = resident.tile([P, 1], F32)
        warm = resident.tile([P, 1], F32)

        nc.vector.memset(ones[:], 1.0)
        nc.vector.memset(eps[:], EPS)
        nc.vector.memset(w_out_planes[:].bitcast(I32), 0)
        nc.vector.memset(gain_bias_row[:].bitcast(I32), 0)
        nc.vector.memset(w_fc1_planes[:].bitcast(I32), 0)
        make_identity(nc, identity[:])
        nc.scalar.activation(out=warm[:], in_=eps[:], func=ACT.Sqrt)

        nc.scalar.dma_start(out=gain_bias_row[0:1, 0:D], in_=g2.rearrange("(o d) -> o d", o=1))
        nc.scalar.dma_start(out=gain_bias_row[0:1, D : 2 * D], in_=b2.rearrange("(o d) -> o d", o=1))
        for m in token_tiles:
            nc.sync.dma_start(out=attn_sb[m][:], in_=attn_in[:, m, :])
        load_scale_planes(nc, w_out_planes, w_out_scales)
        for g in range(PASSES):
            load_weights(nc, w_out_sb, w_out_words, g, 0, BLOCK)
        nc.sync.dma_start(out=x_all[:], in_=x_in)
        for g in range(PASSES - 1):
            load_weights(nc, w_out_sb, w_out_words, g, BLOCK, BLOCK)
        for col0 in range(BLOCK, D, N_TILE):
            load_weights(nc, w_out_sb, w_out_words, PASSES - 1, col0, N_TILE)
        load_scale_planes(nc, w_fc1_planes, w_fc1_scales)
        for col0 in range(0, F, HALF):
            for g in range(PASSES):
                load_weights(nc, w_fc1_sb, w_fc1_words, g, col0, HALF)

        def keep_warm(n):
            unread = flip_banks.tile([P, N_TILE], F32, name="unread", tag="flipped")
            for i in range(n):
                nc.tensor.matmul(out=unread[:], lhsT=ones[:, 0:P], rhs=ones[:], start=True, stop=True)

        keep_warm(4)

        for m in token_tiles:
            for half in range(PASSES // 2):
                grouped = flip(nc, flip_banks, stage, identity, attn_sb[m], half, False)
                quantise(nc, grouped, attn_codes[m], attn_planes[m], half)

        sums = {}

        def out_pass(m, tile, g):
            if g == 0:
                sums[m, tile] = sum_banks.tile([P, N_TILE], F32, name="sums", tag="bank")
            mx_pass(nc, sums[m, tile], g, attn_codes[m], attn_planes[m], w_out_sb, w_out_planes, N_TILE * tile)

        def residual_add(m, tile):
            cols = slice(N_TILE * tile, N_TILE * (tile + 1))
            nc.vector.scalar_tensor_tensor(
                out=x_mid[m][:, cols], in0=sums[m, tile][:], scalar=1.0, in1=x_sb[m][:, cols],
                op0=ALU.mult, op1=ALU.add, accum_out=row_sums[m][:, tile : tile + 1],
            )

        def minus_shift(m):
            nc.vector.tensor_scalar_mul(out=neg_shift[m][:], in0=row_sums[m][:, 0:1], scalar1=-1.0 / N_TILE)

        def squares(m, tile):
            squared = stage.tile([P, N_TILE], BF16, name="squared")
            nc.scalar.activation(
                out=squared[:], in_=x_mid[m][:, N_TILE * tile : N_TILE * (tile + 1)], func=ACT.Square,
                bias=neg_shift[m][:], scale=1.0, accum_out=sq_sums[m][:, tile : tile + 1],
            )

        def first_squares(m):
            scaled = stage.tile([P, D // N_TILE], F32, name="scaled")
            nc.vector.tensor_scalar(
                out=scaled[:, 0:3], in0=sq_sums[m][:, 0:3], scalar1=1.0 / D, scalar2=EPS,
                op0=ALU.mult, op1=ALU.add, accum_out=var_part[m][:],
            )

        def minus_mean(m):
            scaled = stage.tile([P, D // N_TILE], F32, name="scaled")
            nc.vector.tensor_scalar(
                out=scaled[:], in0=row_sums[m][:], scalar1=-1.0 / D, scalar2=None,
                op0=ALU.mult, op1=ALU.add, accum_out=neg_mean[m][:],
            )

        def deviation(m):
            nc.scalar.activation(
                out=shift_sq[m][:], in_=neg_shift[m][:], func=ACT.Square, bias=neg_mean[m][:], scale=-1.0
            )
            nc.scalar.activation(
                out=var_rest[m][:], in_=shift_sq[m][:], func=ACT.Identity, bias=var_part[m][:], scale=-1.0
            )
            nc.scalar.activation(
                out=std[m][:], in_=sq_sums[m][:, 3:4], func=ACT.Sqrt, bias=var_rest[m][:], scale=1.0 / D
            )

        for g in range(PASSES):
            for m in token_tiles:
                for tile in (0, 1):
                    out_pass(m, tile, g)

        def spread(pool, tag, col0):
            bank = pool.tile([P, 2 * N_TILE], BF16, name="spread", tag=tag)
            for i in range(2):
                cols = slice(col0 + N_TILE * i, col0 + N_TILE * (i + 1))
                nc.tensor.matmul(
                    out=in_order(bank[:, N_TILE * i : N_TILE * (i + 1)]),
                    lhsT=ones[:, 0:P],
                    rhs=by_word_half(gain_bias_row[:, cols]),
                    start=True,
                    stop=True,
                )
            return bank

        for col0 in range(0, D, BLOCK):
            bank = spread(flip_banks, "flipped", col0)
            nc.scalar.copy(out=gain[:, col0 : col0 + BLOCK], in_=bank[:])

        for tile in (0, 1):
            for m in token_tiles:
                residual_add(m, tile)
            for m in token_tiles:
                if tile == 0:
                    minus_shift(m)
                squares(m, tile)

        for g in range(PASSES - 1):
            for m in token_tiles:
                for tile in (2, 3):
                    out_pass(m, tile, g)
        for tile in (2, 3):
            for m in token_tiles:
                out_pass(m, tile, PASSES - 1)
        bias = [spread(sum_banks, "bank", D + col0) for col0 in range(0, D, BLOCK)]
        keep_warm(8)

        centred = [stage.tile([P, D], F32, name="centred") for m in token_tiles]

        def centre(m, half, u):
            cols = slice(BLOCK * half, BLOCK * (half + 1))
            natural = x_mid[m][:, cols].rearrange("n (g p u e) -> n u g p e", g=2, u=2, e=2)[:, u]
            split = [
                t[:, cols].rearrange("n (g u p e) -> n u g p e", g=2, u=2, e=2)[:, u] for t in (centred[m], gain)
            ]
            nc.vector.scalar_tensor_tensor(
                out=split[0], in0=natural, scalar=neg_mean[m][:], in1=split[1], op0=ALU.add, op1=ALU.mult
            )

        def normalise(m, half):
            cols = slice(BLOCK * half, BLOCK * (half + 1))
            nc.vector.scalar_tensor_tensor(
                out=h_sb[m][:, cols], in0=centred[m][:, cols], scalar=rstd[m][:], in1=bias[half][:],
                op0=ALU.mult, op1=ALU.add,
            )

        residual_add(0, 2)
        residual_add(1, 2)
        squares(0, 2)
        squares(1, 2)
        residual_add(0, 3)
        squares(0, 3)
        first_squares(0)
        minus_mean(0)
        deviation(0)
        first_squares(1)
        centre(0, 0, 0)
        centre(0, 0, 1)
        centre(0, 1, 0)
        nc.vector.reciprocal(out=rstd[0][:], in_=std[0][:])
        centre(0, 1, 1)
        normalise(0, 0)
        grouped_0 = flip(nc, flip_banks, stage, identity, h_sb[0], 0, True)
        keep_warm(2)
        normalise(0, 1)
        grouped_1 = flip(nc, flip_banks, stage, identity, h_sb[0], 1, True)
        residual_add(1, 3)
        squares(1, 3)
        nc.sync.dma_start(out=x_mid_out, in_=x_mid_all[:])
        quantise(nc, grouped_0, h_codes[0], h_planes[0], 0)
        minus_mean(1)
        deviation(1)
        nc.scalar.activation(out=warm[:], in_=eps[:], func=ACT.Gelu)
        centre(1, 0, 0)
        quantise(nc, grouped_1, h_codes[0], h_planes[0], 1)
        centre(1, 0, 1)
        nc.vector.reciprocal(out=rstd[1][:], in_=std[1][:])
        centre(1, 1, 0)
        centre(1, 1, 1)

        tiles = range(HALF // N_TILE)
        products = {}

        def act_pass(m, half, g, c):
            if g == 0:
                products[m, half, c] = sum_banks.tile([P, N_TILE], F32, name="products", tag="bank")
            mx_pass(
                nc, products[m, half, c], g, h_codes[m], h_planes[m],
                w_fc1_sb, w_fc1_planes, HALF * half + N_TILE * c,
            )

        act_sb = {
            (m, half): resident.tile([P, HALF], F32, name="act_sb%d%d" % (m, half))
            for m in token_tiles
            for half in range(F // HALF)
        }

        def gelu(m, half, c):
            nc.scalar.activation(
                out=act_sb[m, half][:, N_TILE * c : N_TILE * (c + 1)], in_=products[m, half, c][:], func=ACT.Gelu
            )

        def store(m, half, first, last):
            cols = slice(N_TILE * first, N_TILE * (last + 1))
            out_cols = slice(HALF * half + N_TILE * first, HALF * half + N_TILE * (last + 1))
            queue = nc.scalar if m + half == 1 else nc.sync
            queue.dma_start(out=act_out[m][:, out_cols], in_=act_sb[m, half][:, cols])

        pairs = ((0, 1), (2, 3))
        for g in range(PASSES):
            for c in tiles:
                act_pass(0, 0, g, c)
        gelu(0, 0, 0)
        gelu(0, 0, 1)
        normalise(1, 0)
        grouped_0 = flip(nc, flip_banks, stage, identity, h_sb[1], 0, True)
        gelu(0, 0, 2)
        normalise(1, 1)
        grouped_1 = flip(nc, flip_banks, stage, identity, h_sb[1], 1, True)
        gelu(0, 0, 3)
        store(0, 0, 0, 3)
        quantise(nc, grouped_0, h_codes[1], h_planes[1], 0)
        quantise(nc, grouped_1, h_codes[1], h_planes[1], 1)
        for c in (0, 1):
            act_pass(0, 1, 0, c)
        for pair in pairs:
            for g in range(PASSES):
                for c in pair:
                    act_pass(1, 0, g, c)
            for c in pair:
                gelu(1, 0, c)
        store(1, 0, 0, 3)
        for g in range(PASSES):
            for c in tiles:
                if g > 0 or c > 1:
                    act_pass(0, 1, g, c)
        for c in tiles:
            gelu(0, 1, c)
        store(0, 1, 0, 3)
        for pair in pairs:
            for g in range(PASSES):
                for c in pair:
                    act_pass(1, 1, g, c)
            for c in pair:
                gelu(1, 1, c)
                if c != 0:
                    store(1, 1, 0 if c == 1 else c, c)
